import numpy as np
import ml_dtypes


def mxq(x, axis, fmt="e4m3"):
    dtype, down = {"e4m3": (ml_dtypes.float8_e4m3fn, 7), "e5m2": (ml_dtypes.float8_e5m2, 14)}[fmt]
    v = np.moveaxis(np.asarray(x, np.float32).astype(ml_dtypes.bfloat16).astype(np.float64), axis, -1)
    blocks = v.reshape(v.shape[:-1] + (-1, 32))
    amax = np.abs(blocks).max(-1, keepdims=True)
    byte = np.maximum(np.where(amax > 0, np.frexp(amax)[1] - 1 + 127, 0) - down, 1)
    scale = np.exp2(byte - 127.0)
    codes = (blocks / scale).astype(np.float32).astype(dtype).astype(np.float64)
    return np.moveaxis((codes * scale).reshape(v.shape), -1, axis)


WIDE = False


def mx_kscale(k):
    if not WIDE:
        return np.ones(k)
    levels = np.array([10, -10, 5, -5, 0])
    a = np.random.permutation(np.resize(levels, k // 512 * 4)).reshape(k // 512, 4)
    idx = np.arange(k)
    return np.exp2(a[idx // 512, idx % 128 // 32])


BF16 = ml_dtypes.bfloat16


def bf(x):
    return np.asarray(x, np.float32).astype(BF16)


def f64(x):
    return np.asarray(x).astype(np.float64)


B, N1, N2, D, H, FF = 2, 128, 256, 1024, 16, 4096
T = B * (N1 + N2)
D3 = 3 * D
EPS = 1e-5


def layer_norm(x, g, b):
    m = x.mean(-1, keepdims=True)
    v = ((x - m) * (x - m)).mean(-1, keepdims=True)
    return (x - m) * (1.0 / np.sqrt(v + EPS)) * g + b


def setup_inputs():
    s = mx_kscale(D)
    return {"x": bf(np.random.standard_normal((T, D))),
            "ln1_g": bf((1.0 + 0.1 * np.random.standard_normal(D)) * s),
            "ln1_b": bf(0.1 * np.random.standard_normal(D) * s),
            "w_qkv": bf(np.random.standard_normal((D, D3)) * 1.5 / np.sqrt(D) / s[:, None]),
            "b_qkv": bf(0.1 * np.random.standard_normal(D3))}


def reference(x, ln1_g, ln1_b, w_qkv, b_qkv):
    h = layer_norm(f64(x), f64(ln1_g), f64(ln1_b))
    return (mxq(h, 1, "e4m3") @ mxq(f64(w_qkv), 0, "e4m3")) + f64(b_qkv)

@@ -1,0 +1,238 @@
+from contextlib import ExitStack
+
+import concourse.mybir as mybir
+from concourse.masks import make_identity
+
+F32 = mybir.dt.float32
+BF16 = mybir.dt.bfloat16
+U32 = mybir.dt.uint32
+U8 = mybir.dt.uint8
+FP8X4 = mybir.dt.float8_e4m3fn_x4
+ALU = mybir.AluOpType
+ACT = mybir.ActivationFunctionType
+
+P = 128
+PACK = 4
+K_PASS = P * PACK
+TOKENS = 768
+K = 1024
+N = 3072
+EPS = 1e-5
+
+TOKEN_TILES = TOKENS // P
+GROUP_TILES = 3
+GROUPS = TOKEN_TILES // GROUP_TILES
+GROUP_TOKENS = GROUP_TILES * P
+K_PASSES = K // K_PASS
+K_BLOCKS = K // P
+BN_COLS = 512
+CHUNK = 512
+CHUNKS = N // CHUNK
+LOAD_COLS = 1024
+CHUNKS_PER_LOAD = LOAD_COLS // CHUNK
+RUN = 4
+
+FLOPS = 2 * TOKENS * K * N
+
+
+def regroup(copy, grouped, planes):
+    copy(
+        out=grouped.rearrange("p (a i) t -> p a t i", i=RUN),
+        in_=planes.rearrange("p t (a i) -> p a t i", i=RUN),
+    )
+
+
+def tile_nestedtensorblock_pa_kernel(tc, x, ln1_g, ln1_b, w_qkv, b_qkv, out):
+    nc = tc.nc
+    with ExitStack() as ctx:
+        keep = ctx.enter_context(tc.tile_pool(name="keep", bufs=1))
+        stage = ctx.enter_context(tc.tile_pool(name="stage", bufs=3))
+        results = ctx.enter_context(tc.tile_pool(name="results", bufs=6))
+        psum = ctx.enter_context(tc.psum_pool(name="psum", bufs=8))
+        ctx.enter_context(tc.manual_schedule())
+
+        x_sb = keep.tile([P, TOKEN_TILES, K], BF16)
+        w_raw = keep.tile([P, CHUNKS // CHUNKS_PER_LOAD, K_PASSES, PACK, LOAD_COLS], BF16)
+        bias_bc = keep.tile([P, N], BF16)
+        gain_bias_in = keep.tile([2 * K_BLOCKS, P], BF16)
+        gain_bias_rows = keep.tile([P, P], F32)
+        gain_bias = keep.tile([P, 2 * K_BLOCKS], F32)
+        ident = keep.tile([P, P], F32)
+        eps_col = keep.tile([P, 1], F32)
+        warm = keep.tile([P, 1], F32)
+        stats = keep.tile([P, TOKEN_TILES, K // BN_COLS, 6], F32)
+        mean_var = keep.tile([P, TOKEN_TILES, 2], F32)
+        std = keep.tile([P, TOKEN_TILES, 1], F32)
+        rstd = keep.tile([P, TOKEN_TILES, 1], F32)
+        xn = keep.tile([P, TOKEN_TILES, K], F32)
+        h_planes = keep.tile([P, K_BLOCKS, TOKENS], BF16)
+        h_grouped = keep.tile([P, K_PASSES, TOKENS, PACK], BF16, align_bytes=64)
+        h_codes = keep.tile([P, K_PASSES, TOKENS], U32, align_bytes=64)
+        h_scales = keep.tile([P, K_PASSES, TOKENS], U8, align_bytes=64)
+        w_codes = keep.tile([P, CHUNKS, K_PASSES, CHUNK], U32, align_bytes=64)
+        w_scales = keep.tile([P, CHUNKS, K_PASSES, CHUNK], U8, align_bytes=64)
+
+        nc.scalar.dma_start(out=gain_bias_in[0:K_BLOCKS, :], in_=ln1_g.rearrange("(i p) -> i p", p=P))
+        nc.scalar.dma_start(out=gain_bias_in[K_BLOCKS:, :], in_=ln1_b.rearrange("(i p) -> i p", p=P))
+        for i in range(TOKEN_TILES):
+            nc.sync.dma_start(out=x_sb[:, i, :], in_=x[i * P : (i + 1) * P, :])
+
+        def load_w(j):
+            for c in range(K_PASSES):
+                nc.sync.dma_start(
+                    out=w_raw[:, j, c, :, :],
+                    in_=w_qkv[
+                        c * K_PASS : (c + 1) * K_PASS, j * LOAD_COLS : (j + 1) * LOAD_COLS
+                    ].rearrange("(t p) n -> p t n", p=P),
+                )
+
+        load_w(0)
+        nc.sync.dma_start(out=bias_bc[:], in_=b_qkv.partition_broadcast(P))
+        load_w(1)
+        load_w(2)
+
+        make_identity(nc, ident[:])
+        nc.vector.memset(eps_col[:], EPS)
+        nc.vector.memset(gain_bias_rows[:], 0.0)
+        nc.scalar.activation(out=warm[:], in_=eps_col[:], func=ACT.Sqrt)
+
+        nc.vector.tensor_copy(out=gain_bias_rows[0 : 2 * K_BLOCKS, :], in_=gain_bias_in[:])
+        gb_bank = psum.tile([P, CHUNK], F32, tag="bank")
+        nc.tensor.transpose(gb_bank[:, 0:P], gain_bias_rows[:], ident[:])
+        nc.vector.tensor_copy(out=gain_bias[:], in_=gb_bank[:, 0 : 2 * K_BLOCKS])
+
+        def statistics(i):
+            for s in range(K // BN_COLS):
+                nc.vector.bn_stats(
+                    out=stats[:, i, s, :], in_=x_sb[:, i, s * BN_COLS : (s + 1) * BN_COLS]
+                )
+            nc.vector.bn_aggr(
+                out=mean_var[:, i, :], in_=stats[:, i, :, :].rearrange("p s v -> p (s v)")
+            )
+
+        def group_tiles(g):
+            return range(g * GROUP_TILES, (g + 1) * GROUP_TILES)
+
+        def group_sqrt(g):
+            a, b = g * GROUP_TILES, (g + 1) * GROUP_TILES
+            nc.scalar.activation(
+                out=std[:, a:b, :], in_=mean_var[:, a:b, 1:2], func=ACT.Sqrt, bias=eps_col[:, 0:1]
+            )
+
+        def group_normalise(g):
+            a, b = g * GROUP_TILES, (g + 1) * GROUP_TILES
+            nc.vector.reciprocal(out=rstd[:, a:b, :], in_=std[:, a:b, :])
+            for i in group_tiles(g):
+                nc.vector.tensor_scalar(
+                    out=xn[:, i, :],
+                    in0=x_sb[:, i, :],
+                    scalar1=mean_var[:, i, 0:1],
+                    scalar2=rstd[:, i, :],
+                    op0=ALU.subtract,
+                    op1=ALU.mult,
+                )
+
+        def transpose_group(g):
+            tokens = slice(g * GROUP_TOKENS, (g + 1) * GROUP_TOKENS)
+            for kb in range(K_BLOCKS):
+                bank = psum.tile([P, CHUNK], F32, tag="bank")
+                for j in range(GROUP_TILES):
+                    nc.tensor.transpose(
+                        bank[:, j * P : (j + 1) * P],
+                        xn[:, g * GROUP_TILES + j, kb * P : (kb + 1) * P],
+                        ident[:],
+                    )
+                nc.scalar.activation(
+                    out=h_planes[:, kb, tokens],
+                    in_=bank[:, 0:GROUP_TOKENS],
+                    func=ACT.Identity,
+                    bias=gain_bias[:, K_BLOCKS + kb : K_BLOCKS + kb + 1],
+                    scale=gain_bias[:, kb : kb + 1],
+                )
+
+        def regroup_h(g, c):
+            tokens = slice(g * GROUP_TOKENS, (g + 1) * GROUP_TOKENS)
+            regroup(
+                nc.vector.tensor_copy,
+                h_grouped[:, c, tokens, :],
+                h_planes[:, c * PACK : (c + 1) * PACK, tokens],
+            )
+
+        def quantise_h(g, c):
+            for m in group_tiles(g):
+                tokens = slice(m * P, (m + 1) * P)
+                nc.vector.quantize_mx(
+                    out=h_codes[:, c, tokens].bitcast(FP8X4),
+                    scales=h_scales[:, c, tokens],
+                    in_=h_grouped[:, c, tokens, :].rearrange("p n t -> p (n t)"),
+                )
+
+        w_grouped = {}
+
+        def regroup_w(n, c):
+            if c == 0:
+                grouped = stage.tile([P, K_PASSES, CHUNK, PACK], BF16, align_bytes=64, tag="w_grouped")
+                w_grouped[n] = grouped
+            j, half = divmod(n, CHUNKS_PER_LOAD)
+            regroup(
+                nc.scalar.copy,
+                w_grouped[n][:, c, :, :],
+                w_raw[:, j, c, :, half * CHUNK : (half + 1) * CHUNK],
+            )
+
+        def quantise_w(n):
+            nc.vector.quantize_mx(
+                out=w_codes[:, n, :, :].rearrange("p c n -> p (c n)").bitcast(FP8X4),
+                scales=w_scales[:, n, :, :].rearrange("p c n -> p (c n)"),
+                in_=w_grouped[n][:].rearrange("p c n t -> p (c n t)"),
+            )
+
+        def multiply(n, m):
+            tokens = slice(m * P, (m + 1) * P)
+            cols = slice(n * CHUNK, (n + 1) * CHUNK)
+            acc = psum.tile([P, CHUNK], F32, tag="bank")
+            for c in range(K_PASSES):
+                nc.tensor.matmul_mx(
+                    out=acc[:],
+                    lhsT=h_codes[:, c, tokens].bitcast(FP8X4),
+                    lhsT_scale=h_scales[:, c, tokens],
+                    rhs=w_codes[:, n, c, :].bitcast(FP8X4),
+                    rhs_scale=w_scales[:, n, c, :],
+                    start=(c == 0),
+                    stop=(c == K_PASSES - 1),
+                )
+            result = results.tile([P, CHUNK], F32)
+            nc.vector.tensor_tensor(out=result[:], in0=acc[:], in1=bias_bc[:, cols], op=ALU.add)
+            nc.sync.dma_start(out=out[tokens, cols], in_=result[:])
+
+        for i in group_tiles(0):
+            statistics(i)
+        group_sqrt(0)
+        for i in group_tiles(1):
+            statistics(i)
+        regroup_w(0, 0)
+        group_sqrt(1)
+        group_normalise(0)
+        group_normalise(1)
+        regroup_w(0, 1)
+        transpose_group(0)
+        transpose_group(1)
+
+        regroup_h(0, 0)
+        quantise_w(0)
+        regroup_h(0, 1)
+        quantise_h(0, 0)
+        regroup_h(1, 0)
+        quantise_h(0, 1)
+        regroup_h(1, 1)
+        quantise_h(1, 0)
+        quantise_h(1, 1)
+
+        for n in range(CHUNKS):
+            if n + 1 < CHUNKS:
+                regroup_w(n + 1, 0)
+                regroup_w(n + 1, 1)
+            for m in range(TOKEN_TILES):
+                multiply(n, m)
+                if m == TOKEN_TILES - 3 and n + 1 < CHUNKS:
+                    quantise_w(n + 1)

@@ -49,7 +49,6 @@ def tile_nestedtensorblock_pa_kernel(tc, x, ln1_g, ln1_b, w_qkv, b_qkv, out):
         stage = ctx.enter_context(tc.tile_pool(name="stage", bufs=3))
         results = ctx.enter_context(tc.tile_pool(name="results", bufs=6))
         psum = ctx.enter_context(tc.psum_pool(name="psum", bufs=8))
-        ctx.enter_context(tc.manual_schedule())
 
         x_sb = keep.tile([P, TOKEN_TILES, K], BF16)
         w_raw = keep.tile([P, CHUNKS // CHUNKS_PER_LOAD, K_PASSES, PACK, LOAD_COLS], BF16)

@@ -47,7 +47,7 @@ def tile_nestedtensorblock_pa_kernel(tc, x, ln1_g, ln1_b, w_qkv, b_qkv, out):
     with ExitStack() as ctx:
         keep = ctx.enter_context(tc.tile_pool(name="keep", bufs=1))
         stage = ctx.enter_context(tc.tile_pool(name="stage", bufs=3))
-        results = ctx.enter_context(tc.tile_pool(name="results", bufs=6))
+        results = ctx.enter_context(tc.tile_pool(name="results", bufs=12))
         psum = ctx.enter_context(tc.psum_pool(name="psum", bufs=8))
 
         x_sb = keep.tile([P, TOKEN_TILES, K], BF16)

@@ -30,7 +30,12 @@ CHUNK = 512
 CHUNKS = N // CHUNK
 LOAD_COLS = 1024
 CHUNKS_PER_LOAD = LOAD_COLS // CHUNK
+SCALAR_TILES = 2
+VECTOR_CHUNKS = 1
 RUN = 4
+
+VECTOR_TILES = TOKEN_TILES - SCALAR_TILES
+TILE_ORDER = [0, VECTOR_TILES, 1, VECTOR_TILES + 1, 2, 3]
 
 FLOPS = 2 * TOKENS * K * N
 
@@ -47,7 +52,7 @@ def tile_nestedtensorblock_pa_kernel(tc, x, ln1_g, ln1_b, w_qkv, b_qkv, out):
     with ExitStack() as ctx:
         keep = ctx.enter_context(tc.tile_pool(name="keep", bufs=1))
         stage = ctx.enter_context(tc.tile_pool(name="stage", bufs=3))
-        results = ctx.enter_context(tc.tile_pool(name="results", bufs=12))
+        results = ctx.enter_context(tc.tile_pool(name="results", bufs=6))
         psum = ctx.enter_context(tc.psum_pool(name="psum", bufs=8))
 
         x_sb = keep.tile([P, TOKEN_TILES, K], BF16)
@@ -63,6 +68,10 @@ def tile_nestedtensorblock_pa_kernel(tc, x, ln1_g, ln1_b, w_qkv, b_qkv, out):
         mean_var = keep.tile([P, TOKEN_TILES, 2], F32)
         std = keep.tile([P, TOKEN_TILES, 1], F32)
         rstd = keep.tile([P, TOKEN_TILES, 1], F32)
+        total = keep.tile([P, TOKEN_TILES, 1], F32)
+        neg_mean = keep.tile([P, TOKEN_TILES, 1], F32)
+        sum_sq = keep.tile([P, TOKEN_TILES, 1], F32)
+        unread = keep.tile([P, SCALAR_TILES, 2, K], BF16)
         xn = keep.tile([P, TOKEN_TILES, K], F32)
         h_planes = keep.tile([P, K_BLOCKS, TOKENS], BF16)
         h_grouped = keep.tile([P, K_PASSES, TOKENS, PACK], BF16, align_bytes=64)
@@ -73,7 +82,7 @@ def tile_nestedtensorblock_pa_kernel(tc, x, ln1_g, ln1_b, w_qkv, b_qkv, out):
 
         nc.scalar.dma_start(out=gain_bias_in[0:K_BLOCKS, :], in_=ln1_g.rearrange("(i p) -> i p", p=P))
         nc.scalar.dma_start(out=gain_bias_in[K_BLOCKS:, :], in_=ln1_b.rearrange("(i p) -> i p", p=P))
-        for i in range(TOKEN_TILES):
+        for i in TILE_ORDER:
             nc.sync.dma_start(out=x_sb[:, i, :], in_=x[i * P : (i + 1) * P, :])
 
         def load_w(j):
@@ -100,7 +109,10 @@ def tile_nestedtensorblock_pa_kernel(tc, x, ln1_g, ln1_b, w_qkv, b_qkv, out):
         nc.tensor.transpose(gb_bank[:, 0:P], gain_bias_rows[:], ident[:])
         nc.vector.tensor_copy(out=gain_bias[:], in_=gb_bank[:, 0 : 2 * K_BLOCKS])
 
-        def statistics(i):
+        def group_tiles(g):
+            return range(g * GROUP_TILES, (g + 1) * GROUP_TILES)
+
+        def normalise_on_vector(i):
             for s in range(K // BN_COLS):
                 nc.vector.bn_stats(
                     out=stats[:, i, s, :], in_=x_sb[:, i, s * BN_COLS : (s + 1) * BN_COLS]
@@ -108,28 +120,52 @@ def tile_nestedtensorblock_pa_kernel(tc, x, ln1_g, ln1_b, w_qkv, b_qkv, out):
             nc.vector.bn_aggr(
                 out=mean_var[:, i, :], in_=stats[:, i, :, :].rearrange("p s v -> p (s v)")
             )
-
-        def group_tiles(g):
-            return range(g * GROUP_TILES, (g + 1) * GROUP_TILES)
-
-        def group_sqrt(g):
-            a, b = g * GROUP_TILES, (g + 1) * GROUP_TILES
             nc.scalar.activation(
-                out=std[:, a:b, :], in_=mean_var[:, a:b, 1:2], func=ACT.Sqrt, bias=eps_col[:, 0:1]
+                out=std[:, i, :], in_=mean_var[:, i, 1:2], func=ACT.Sqrt, bias=eps_col[:, 0:1]
+            )
+            nc.vector.reciprocal(out=rstd[:, i, :], in_=std[:, i, :])
+            nc.vector.tensor_scalar(
+                out=xn[:, i, :],
+                in0=x_sb[:, i, :],
+                scalar1=mean_var[:, i, 0:1],
+                scalar2=rstd[:, i, :],
+                op0=ALU.subtract,
+                op1=ALU.mult,
             )
 
-        def group_normalise(g):
-            a, b = g * GROUP_TILES, (g + 1) * GROUP_TILES
-            nc.vector.reciprocal(out=rstd[:, a:b, :], in_=std[:, a:b, :])
-            for i in group_tiles(g):
-                nc.vector.tensor_scalar(
-                    out=xn[:, i, :],
-                    in0=x_sb[:, i, :],
-                    scalar1=mean_var[:, i, 0:1],
-                    scalar2=rstd[:, i, :],
-                    op0=ALU.subtract,
-                    op1=ALU.mult,
-                )
+        def statistics_on_scalar(i):
+            spare = unread[:, i - VECTOR_TILES, :, :]
+            nc.scalar.activation(
+                out=spare[:, 0, :], in_=x_sb[:, i, :], func=ACT.Identity, accum_out=total[:, i, :]
+            )
+            nc.scalar.activation(
+                out=neg_mean[:, i, :], in_=total[:, i, :], func=ACT.Copy, scale=-1.0 / K
+            )
+            nc.scalar.activation(
+                out=spare[:, 1, :],
+                in_=x_sb[:, i, :],
+                func=ACT.Square,
+                bias=neg_mean[:, i, :],
+                accum_out=sum_sq[:, i, :],
+            )
+            nc.scalar.activation(
+                out=std[:, i, :],
+                in_=sum_sq[:, i, :],
+                func=ACT.Sqrt,
+                bias=eps_col[:, 0:1],
+                scale=1.0 / K,
+            )
+            nc.vector.reciprocal(out=rstd[:, i, :], in_=std[:, i, :])
+
+        def normalise_after_scalar(i):
+            nc.vector.tensor_scalar(
+                out=xn[:, i, :],
+                in0=x_sb[:, i, :],
+                scalar1=neg_mean[:, i, :],
+                scalar2=rstd[:, i, :],
+                op0=ALU.add,
+                op1=ALU.mult,
+            )
 
         def transpose_group(g):
             tokens = slice(g * GROUP_TOKENS, (g + 1) * GROUP_TOKENS)
@@ -174,7 +210,7 @@ def tile_nestedtensorblock_pa_kernel(tc, x, ln1_g, ln1_b, w_qkv, b_qkv, out):
                 w_grouped[n] = grouped
             j, half = divmod(n, CHUNKS_PER_LOAD)
             regroup(
-                nc.scalar.copy,
+                nc.vector.tensor_copy if n < VECTOR_CHUNKS else nc.scalar.copy,
                 w_grouped[n][:, c, :, :],
                 w_raw[:, j, c, :, half * CHUNK : (half + 1) * CHUNK],
             )
@@ -204,15 +240,14 @@ def tile_nestedtensorblock_pa_kernel(tc, x, ln1_g, ln1_b, w_qkv, b_qkv, out):
             nc.vector.tensor_tensor(out=result[:], in0=acc[:], in1=bias_bc[:, cols], op=ALU.add)
             nc.sync.dma_start(out=out[tokens, cols], in_=result[:])
 
-        for i in group_tiles(0):
-            statistics(i)
-        group_sqrt(0)
-        for i in group_tiles(1):
-            statistics(i)
+        for i in TILE_ORDER:
+            if i < VECTOR_TILES:
+                normalise_on_vector(i)
+            else:
+                statistics_on_scalar(i)
+        for i in range(VECTOR_TILES, TOKEN_TILES):
+            normalise_after_scalar(i)
         regroup_w(0, 0)
-        group_sqrt(1)
-        group_normalise(0)
-        group_normalise(1)
         regroup_w(0, 1)
         transpose_group(0)
         transpose_group(1)

@@ -20,9 +20,9 @@ N = 3072
 EPS = 1e-5
 
 TOKEN_TILES = TOKENS // P
-GROUP_TILES = 3
-GROUPS = TOKEN_TILES // GROUP_TILES
-GROUP_TOKENS = GROUP_TILES * P
+PAIR = 2
+GROUPS = TOKEN_TILES // PAIR
+GROUP_TOKENS = PAIR * P
 K_PASSES = K // K_PASS
 K_BLOCKS = K // P
 BN_COLS = 512
@@ -30,12 +30,16 @@ CHUNK = 512
 CHUNKS = N // CHUNK
 LOAD_COLS = 1024
 CHUNKS_PER_LOAD = LOAD_COLS // CHUNK
-SCALAR_TILES = 2
-VECTOR_CHUNKS = 1
 RUN = 4
 
-VECTOR_TILES = TOKEN_TILES - SCALAR_TILES
-TILE_ORDER = [0, VECTOR_TILES, 1, VECTOR_TILES + 1, 2, 3]
+SCALAR_STATS = [1, 3]
+GPSIMD_NORM = []
+W_ENGINE = "vsssgs"
+G_COLS = 128
+SCALAR_BANKS = [(4, 1), (4, 4), (5, 1), (5, 3)]
+STORE_LAG = 3
+QUANT_AT = 2
+W_LOADS = [(0, 1), (1, 1), (2, 2), (4, 2)]
 
 FLOPS = 2 * TOKENS * K * N
 
@@ -51,12 +55,13 @@ def tile_nestedtensorblock_pa_kernel(tc, x, ln1_g, ln1_b, w_qkv, b_qkv, out):
     nc = tc.nc
     with ExitStack() as ctx:
         keep = ctx.enter_context(tc.tile_pool(name="keep", bufs=1))
-        stage = ctx.enter_context(tc.tile_pool(name="stage", bufs=3))
-        results = ctx.enter_context(tc.tile_pool(name="results", bufs=6))
+        stage = ctx.enter_context(tc.tile_pool(name="stage", bufs=4))
+        results = ctx.enter_context(tc.tile_pool(name="results", bufs=14))
+        sums = ctx.enter_context(tc.tile_pool(name="sums", bufs=4))
         psum = ctx.enter_context(tc.psum_pool(name="psum", bufs=8))
 
         x_sb = keep.tile([P, TOKEN_TILES, K], BF16)
-        w_raw = keep.tile([P, CHUNKS // CHUNKS_PER_LOAD, K_PASSES, PACK, LOAD_COLS], BF16)
+        w_raw = {}
         bias_bc = keep.tile([P, N], BF16)
         gain_bias_in = keep.tile([2 * K_BLOCKS, P], BF16)
         gain_bias_rows = keep.tile([P, P], F32)
@@ -65,155 +70,165 @@ def tile_nestedtensorblock_pa_kernel(tc, x, ln1_g, ln1_b, w_qkv, b_qkv, out):
         eps_col = keep.tile([P, 1], F32)
         warm = keep.tile([P, 1], F32)
         stats = keep.tile([P, TOKEN_TILES, K // BN_COLS, 6], F32)
-        mean_var = keep.tile([P, TOKEN_TILES, 2], F32)
-        std = keep.tile([P, TOKEN_TILES, 1], F32)
-        rstd = keep.tile([P, TOKEN_TILES, 1], F32)
-        total = keep.tile([P, TOKEN_TILES, 1], F32)
-        neg_mean = keep.tile([P, TOKEN_TILES, 1], F32)
-        sum_sq = keep.tile([P, TOKEN_TILES, 1], F32)
-        unread = keep.tile([P, SCALAR_TILES, 2, K], BF16)
+        mean_var = keep.tile([P, TOKEN_TILES, 8], F32)
+        rstd = keep.tile([P, TOKEN_TILES, 8], F32)
+        total = keep.tile([P, TOKEN_TILES, 8], F32)
+        neg_mean = keep.tile([P, TOKEN_TILES, 8], F32)
+        sum_sq = keep.tile([P, TOKEN_TILES, 8], F32)
+        unread = keep.tile([P, len(SCALAR_STATS), 2, K], BF16)
         xn = keep.tile([P, TOKEN_TILES, K], F32)
         h_planes = keep.tile([P, K_BLOCKS, TOKENS], BF16)
-        h_grouped = keep.tile([P, K_PASSES, TOKENS, PACK], BF16, align_bytes=64)
-        h_codes = keep.tile([P, K_PASSES, TOKENS], U32, align_bytes=64)
-        h_scales = keep.tile([P, K_PASSES, TOKENS], U8, align_bytes=64)
+        h_grouped = keep.tile([P, GROUPS, K_PASSES, GROUP_TOKENS, PACK], BF16, align_bytes=64)
+        h_codes = keep.tile([P, GROUPS, K_PASSES, GROUP_TOKENS], U32, align_bytes=64)
+        h_scales = keep.tile([P, GROUPS, K_PASSES, GROUP_TOKENS], U8, align_bytes=64)
         w_codes = keep.tile([P, CHUNKS, K_PASSES, CHUNK], U32, align_bytes=64)
         w_scales = keep.tile([P, CHUNKS, K_PASSES, CHUNK], U8, align_bytes=64)
 
-        nc.scalar.dma_start(out=gain_bias_in[0:K_BLOCKS, :], in_=ln1_g.rearrange("(i p) -> i p", p=P))
-        nc.scalar.dma_start(out=gain_bias_in[K_BLOCKS:, :], in_=ln1_b.rearrange("(i p) -> i p", p=P))
-        for i in TILE_ORDER:
+        def load_x(i):
             nc.sync.dma_start(out=x_sb[:, i, :], in_=x[i * P : (i + 1) * P, :])
 
-        def load_w(j):
-            for c in range(K_PASSES):
+        def load_w(first, chunks, passes):
+            if first not in w_raw:
+                raw = keep.tile([P, K_PASSES, PACK, chunks * CHUNK], BF16, name="raw_%d" % first)
+                for n in range(chunks):
+                    w_raw[first + n] = (raw, n * CHUNK)
+            raw = w_raw[first][0]
+            for c in passes:
                 nc.sync.dma_start(
-                    out=w_raw[:, j, c, :, :],
+                    out=raw[:, c, :, :],
                     in_=w_qkv[
-                        c * K_PASS : (c + 1) * K_PASS, j * LOAD_COLS : (j + 1) * LOAD_COLS
+                        c * K_PASS : (c + 1) * K_PASS, first * CHUNK : (first + chunks) * CHUNK
                     ].rearrange("(t p) n -> p t n", p=P),
                 )
 
-        load_w(0)
+        nc.scalar.dma_start(out=gain_bias_in[0:K_BLOCKS, :], in_=ln1_g.rearrange("(i p) -> i p", p=P))
+        nc.scalar.dma_start(out=gain_bias_in[K_BLOCKS:, :], in_=ln1_b.rearrange("(i p) -> i p", p=P))
+        load_x(0)
+        load_x(1)
+        load_x(2)
+        load_x(3)
+        load_x(4)
+        load_x(5)
+        load_w(0, 1, [0, 1])
+        load_w(1, 1, [0, 1])
         nc.sync.dma_start(out=bias_bc[:], in_=b_qkv.partition_broadcast(P))
-        load_w(1)
-        load_w(2)
+        load_w(2, 2, [0, 1])
+        load_w(4, 2, [0, 1])
 
-        make_identity(nc, ident[:])
         nc.vector.memset(eps_col[:], EPS)
         nc.vector.memset(gain_bias_rows[:], 0.0)
-        nc.scalar.activation(out=warm[:], in_=eps_col[:], func=ACT.Sqrt)
+        nc.scalar.activation(out=warm[:], in_=eps_col[:], func=ACT.Abs_reciprocal_sqrt)
+        make_identity(nc, ident[:])
 
-        nc.vector.tensor_copy(out=gain_bias_rows[0 : 2 * K_BLOCKS, :], in_=gain_bias_in[:])
-        gb_bank = psum.tile([P, CHUNK], F32, tag="bank")
-        nc.tensor.transpose(gb_bank[:, 0:P], gain_bias_rows[:], ident[:])
-        nc.vector.tensor_copy(out=gain_bias[:], in_=gb_bank[:, 0 : 2 * K_BLOCKS])
+        def spread_gain_and_bias():
+            nc.vector.tensor_copy(out=gain_bias_rows[0 : 2 * K_BLOCKS, :], in_=gain_bias_in[:])
+            gb_bank = psum.tile([P, CHUNK], F32, tag="bank")
+            nc.tensor.transpose(gb_bank[:, 0:P], gain_bias_rows[:], ident[:])
+            nc.scalar.copy(out=gain_bias[:], in_=gb_bank[:, 0 : 2 * K_BLOCKS])
 
-        def group_tiles(g):
-            return range(g * GROUP_TILES, (g + 1) * GROUP_TILES)
+        def statistics(i, s):
+            nc.vector.bn_stats(out=stats[:, i, s, :], in_=x_sb[:, i, s * BN_COLS : (s + 1) * BN_COLS])
 
-        def normalise_on_vector(i):
-            for s in range(K // BN_COLS):
-                nc.vector.bn_stats(
-                    out=stats[:, i, s, :], in_=x_sb[:, i, s * BN_COLS : (s + 1) * BN_COLS]
-                )
+        def aggregate(i):
             nc.vector.bn_aggr(
-                out=mean_var[:, i, :], in_=stats[:, i, :, :].rearrange("p s v -> p (s v)")
-            )
-            nc.scalar.activation(
-                out=std[:, i, :], in_=mean_var[:, i, 1:2], func=ACT.Sqrt, bias=eps_col[:, 0:1]
-            )
-            nc.vector.reciprocal(out=rstd[:, i, :], in_=std[:, i, :])
-            nc.vector.tensor_scalar(
-                out=xn[:, i, :],
-                in0=x_sb[:, i, :],
-                scalar1=mean_var[:, i, 0:1],
-                scalar2=rstd[:, i, :],
-                op0=ALU.subtract,
-                op1=ALU.mult,
+                out=mean_var[:, i, 0:2], in_=stats[:, i, :, :].rearrange("p s v -> p (s v)")
             )
 
-        def statistics_on_scalar(i):
-            spare = unread[:, i - VECTOR_TILES, :, :]
+        def root(i):
+            own = i in SCALAR_STATS
             nc.scalar.activation(
-                out=spare[:, 0, :], in_=x_sb[:, i, :], func=ACT.Identity, accum_out=total[:, i, :]
+                out=rstd[:, i, 0:1],
+                in_=sum_sq[:, i, 0:1] if own else mean_var[:, i, 1:2],
+                func=ACT.Abs_reciprocal_sqrt,
+                bias=eps_col[:, 0:1],
+                scale=1.0 / K if own else 1.0,
+            )
+
+        def scalar_sum(i):
+            nc.scalar.activation(
+                out=unread[:, SCALAR_STATS.index(i), 0, :],
+                in_=x_sb[:, i, :],
+                func=ACT.Identity,
+                accum_out=total[:, i, 0:1],
             )
             nc.scalar.activation(
-                out=neg_mean[:, i, :], in_=total[:, i, :], func=ACT.Copy, scale=-1.0 / K
+                out=neg_mean[:, i, 0:1], in_=total[:, i, 0:1], func=ACT.Copy, scale=-1.0 / K
             )
+
+        def scalar_squares(i):
             nc.scalar.activation(
-                out=spare[:, 1, :],
+                out=unread[:, SCALAR_STATS.index(i), 1, :],
                 in_=x_sb[:, i, :],
                 func=ACT.Square,
-                bias=neg_mean[:, i, :],
-                accum_out=sum_sq[:, i, :],
+                bias=neg_mean[:, i, 0:1],
+                accum_out=sum_sq[:, i, 0:1],
             )
-            nc.scalar.activation(
-                out=std[:, i, :],
-                in_=sum_sq[:, i, :],
-                func=ACT.Sqrt,
-                bias=eps_col[:, 0:1],
-                scale=1.0 / K,
-            )
-            nc.vector.reciprocal(out=rstd[:, i, :], in_=std[:, i, :])
 
-        def normalise_after_scalar(i):
-            nc.vector.tensor_scalar(
+        def normalise(i):
+            engine = nc.gpsimd if i in GPSIMD_NORM else nc.vector
+            own = i in SCALAR_STATS
+            engine.tensor_scalar(
                 out=xn[:, i, :],
                 in0=x_sb[:, i, :],
-                scalar1=neg_mean[:, i, :],
-                scalar2=rstd[:, i, :],
-                op0=ALU.add,
+                scalar1=neg_mean[:, i, 0:1] if own else mean_var[:, i, 0:1],
+                scalar2=rstd[:, i, 0:1],
+                op0=ALU.add if own else ALU.subtract,
                 op1=ALU.mult,
             )
 
-        def transpose_group(g):
-            tokens = slice(g * GROUP_TOKENS, (g + 1) * GROUP_TOKENS)
-            for kb in range(K_BLOCKS):
+        h_banks = {}
+
+        def transpose(g):
+            for kb in range(0, K_BLOCKS, 2):
                 bank = psum.tile([P, CHUNK], F32, tag="bank")
-                for j in range(GROUP_TILES):
-                    nc.tensor.transpose(
-                        bank[:, j * P : (j + 1) * P],
-                        xn[:, g * GROUP_TILES + j, kb * P : (kb + 1) * P],
-                        ident[:],
-                    )
-                nc.scalar.activation(
-                    out=h_planes[:, kb, tokens],
-                    in_=bank[:, 0:GROUP_TOKENS],
-                    func=ACT.Identity,
-                    bias=gain_bias[:, K_BLOCKS + kb : K_BLOCKS + kb + 1],
-                    scale=gain_bias[:, kb : kb + 1],
-                )
+                h_banks[(g, kb)] = bank
+                for b in range(2):
+                    for j in range(PAIR):
+                        nc.tensor.transpose(
+                            bank[:, (b * PAIR + j) * P : (b * PAIR + j + 1) * P],
+                            xn[:, g * PAIR + j, (kb + b) * P : (kb + b + 1) * P],
+                            ident[:],
+                        )
+
+        def bring_out(g, c):
+            for k in range(c * PACK, (c + 1) * PACK):
+                o = h_planes[:, k, g * GROUP_TOKENS : (g + 1) * GROUP_TOKENS]
+                half = (k % 2) * GROUP_TOKENS
+                i = h_banks[(g, k - k % 2)][:, half : half + GROUP_TOKENS]
+                gain = gain_bias[:, k : k + 1]
+                bias = gain_bias[:, K_BLOCKS + k : K_BLOCKS + k + 1]
+                nc.scalar.activation(out=o, in_=i, func=ACT.Identity, bias=bias, scale=gain)
 
         def regroup_h(g, c):
-            tokens = slice(g * GROUP_TOKENS, (g + 1) * GROUP_TOKENS)
             regroup(
                 nc.vector.tensor_copy,
-                h_grouped[:, c, tokens, :],
-                h_planes[:, c * PACK : (c + 1) * PACK, tokens],
+                h_grouped[:, g, c, :, :],
+                h_planes[:, c * PACK : (c + 1) * PACK, g * GROUP_TOKENS : (g + 1) * GROUP_TOKENS],
             )
 
-        def quantise_h(g, c):
-            for m in group_tiles(g):
-                tokens = slice(m * P, (m + 1) * P)
-                nc.vector.quantize_mx(
-                    out=h_codes[:, c, tokens].bitcast(FP8X4),
-                    scales=h_scales[:, c, tokens],
-                    in_=h_grouped[:, c, tokens, :].rearrange("p n t -> p (n t)"),
-                )
+        def quantise_h(g):
+            nc.vector.quantize_mx(
+                out=h_codes[:, g, :, :].rearrange("p c n -> p (c n)").bitcast(FP8X4),
+                scales=h_scales[:, g, :, :].rearrange("p c n -> p (c n)"),
+                in_=h_grouped[:, g, :, :, :].rearrange("p c n t -> p (c n t)"),
+            )
 
         w_grouped = {}
 
-        def regroup_w(n, c):
-            if c == 0:
+        def copy_on_gpsimd(out, in_):
+            nc.gpsimd.tensor_scalar(out=out, in0=in_, scalar1=1.0, scalar2=0.0, op0=ALU.mult, op1=ALU.add)
+
+        def regroup_w(n, c, pieces=None):
+            if n not in w_grouped:
                 grouped = stage.tile([P, K_PASSES, CHUNK, PACK], BF16, align_bytes=64, tag="w_grouped")
                 w_grouped[n] = grouped
-            j, half = divmod(n, CHUNKS_PER_LOAD)
-            regroup(
-                nc.vector.tensor_copy if n < VECTOR_CHUNKS else nc.scalar.copy,
-                w_grouped[n][:, c, :, :],
-                w_raw[:, j, c, :, half * CHUNK : (half + 1) * CHUNK],
-            )
+            raw, first = w_raw[n]
+            e = W_ENGINE[n]
+            copy = {"v": nc.vector.tensor_copy, "s": nc.scalar.copy, "g": copy_on_gpsimd}[e]
+            width = G_COLS if e == "g" else CHUNK
+            for i, q in enumerate(range(0, CHUNK, width)):
+                if pieces is None or i in pieces:
+                    regroup(copy, w_grouped[n][:, c, q : q + width, :], raw[:, c, :, first + q : first + q + width])
 
         def quantise_w(n):
             nc.vector.quantize_mx(
@@ -222,51 +237,112 @@ def tile_nestedtensorblock_pa_kernel(tc, x, ln1_g, ln1_b, w_qkv, b_qkv, out):
                 in_=w_grouped[n][:].rearrange("p c n t -> p (c n t)"),
             )
 
+        waiting = []
+
+        def store(n, m, result):
+            nc.sync.dma_start(
+                out=out[m * P : (m + 1) * P, n * CHUNK : (n + 1) * CHUNK], in_=result[:]
+            )
+
         def multiply(n, m):
-            tokens = slice(m * P, (m + 1) * P)
+            g, j = divmod(m, PAIR)
+            tokens = slice(j * P, (j + 1) * P)
             cols = slice(n * CHUNK, (n + 1) * CHUNK)
             acc = psum.tile([P, CHUNK], F32, tag="bank")
             for c in range(K_PASSES):
                 nc.tensor.matmul_mx(
                     out=acc[:],
-                    lhsT=h_codes[:, c, tokens].bitcast(FP8X4),
-                    lhsT_scale=h_scales[:, c, tokens],
+                    lhsT=h_codes[:, g, c, tokens].bitcast(FP8X4),
+                    lhsT_scale=h_scales[:, g, c, tokens],
                     rhs=w_codes[:, n, c, :].bitcast(FP8X4),
                     rhs_scale=w_scales[:, n, c, :],
                     start=(c == 0),
                     stop=(c == K_PASSES - 1),
                 )
             result = results.tile([P, CHUNK], F32)
-            nc.vector.tensor_tensor(out=result[:], in0=acc[:], in1=bias_bc[:, cols], op=ALU.add)
-            nc.sync.dma_start(out=out[tokens, cols], in_=result[:])
-
-        for i in TILE_ORDER:
-            if i < VECTOR_TILES:
-                normalise_on_vector(i)
+            if (n, m) in SCALAR_BANKS:
+                plain = sums.tile([P, CHUNK], F32)
+                nc.scalar.copy(out=plain[:], in_=acc[:])
+                nc.gpsimd.tensor_tensor(out=result[:], in0=plain[:], in1=bias_bc[:, cols], op=ALU.add)
+                waiting.append([STORE_LAG, n, m, result])
             else:
-                statistics_on_scalar(i)
-        for i in range(VECTOR_TILES, TOKEN_TILES):
-            normalise_after_scalar(i)
-        regroup_w(0, 0)
-        regroup_w(0, 1)
-        transpose_group(0)
-        transpose_group(1)
+                nc.vector.tensor_tensor(out=result[:], in0=acc[:], in1=bias_bc[:, cols], op=ALU.add)
+                store(n, m, result)
+            for w in list(waiting):
+                w[0] -= 1
+                if w[0] < 0 or (n, m) == (CHUNKS - 1, TOKEN_TILES - 1):
+                    store(*w[1:])
+                    waiting.remove(w)
 
+        def both_statistics(i):
+            for s in range(K // BN_COLS):
+                statistics(i, s)
+
+        both_statistics(0)
+        scalar_sum(1)
+        aggregate(0)
+        root(0)
+        normalise(0)
+        both_statistics(2)
+        spread_gain_and_bias()
+        scalar_squares(1)
+        root(1)
+        statistics(4, 0)
+        aggregate(2)
+        root(2)
+        normalise(2)
+        statistics(4, 1)
+        normalise(1)
+        transpose(0)
+        scalar_sum(3)
+        statistics(5, 0)
+        aggregate(4)
+        statistics(5, 1)
+        root(4)
+        normalise(4)
+        scalar_squares(3)
+        regroup_w(0, 0)
+        aggregate(5)
+        root(3)
+        root(5)
+        regroup_w(0, 1)
+        normalise(3)
+        normalise(5)
+        bring_out(0, 0)
+        transpose(1)
+        bring_out(0, 1)
+        transpose(2)
         regroup_h(0, 0)
         quantise_w(0)
         regroup_h(0, 1)
-        quantise_h(0, 0)
+        bring_out(1, 0)
+        bring_out(1, 1)
+        bring_out(2, 0)
+        bring_out(2, 1)
+        regroup_w(1, 0)
+        regroup_w(1, 1)
         regroup_h(1, 0)
-        quantise_h(0, 1)
+        quantise_h(0)
         regroup_h(1, 1)
-        quantise_h(1, 0)
-        quantise_h(1, 1)
-
-        for n in range(CHUNKS):
-            if n + 1 < CHUNKS:
-                regroup_w(n + 1, 0)
-                regroup_w(n + 1, 1)
+        multiply(0, 0)
+        quantise_h(1)
+        multiply(0, 1)
+        regroup_h(2, 0)
+        regroup_h(2, 1)
+        multiply(0, 2)
+        quantise_h(2)
+        multiply(0, 3)
+        multiply(0, 4)
+        quantise_w(1)
+        multiply(0, 5)
+        for n in (2, 3):
+            regroup_w(n, 0)
+            regroup_w(n, 1)
+        for n in (4, 5):
+            regroup_w(n, 0)
+            regroup_w(n, 1)
+        for n in range(1, CHUNKS):
             for m in range(TOKEN_TILES):
                 multiply(n, m)
-                if m == TOKEN_TILES - 3 and n + 1 < CHUNKS:
+                if m == QUANT_AT and n + 1 < CHUNKS:
                     quantise_w(n + 1)

@@ -36,8 +36,8 @@ SCALAR_STATS = [1, 3]
 GPSIMD_NORM = []
 W_ENGINE = "vsssgs"
 G_COLS = 128
-SCALAR_BANKS = [(4, 1), (4, 4), (5, 1), (5, 3)]
-STORE_LAG = 3
+SCALAR_BANKS = [(3, 2), (3, 5), (4, 1), (4, 4), (5, 0), (5, 2)]
+STORE_LAG = 2
 QUANT_AT = 2
 W_LOADS = [(0, 1), (1, 1), (2, 2), (4, 2)]
 
@@ -216,7 +216,7 @@ def tile_nestedtensorblock_pa_kernel(tc, x, ln1_g, ln1_b, w_qkv, b_qkv, out):
         w_grouped = {}
 
         def copy_on_gpsimd(out, in_):
-            nc.gpsimd.tensor_scalar(out=out, in0=in_, scalar1=1.0, scalar2=0.0, op0=ALU.mult, op1=ALU.add)
+            nc.gpsimd.tensor_copy(out=out, in_=in_)
 
         def regroup_w(n, c, pieces=None):
             if n not in w_grouped:
@@ -301,13 +301,13 @@ def tile_nestedtensorblock_pa_kernel(tc, x, ln1_g, ln1_b, w_qkv, b_qkv, out):
         root(4)
         normalise(4)
         scalar_squares(3)
-        regroup_w(0, 0)
         aggregate(5)
         root(3)
         root(5)
-        regroup_w(0, 1)
         normalise(3)
         normalise(5)
+        regroup_w(0, 0)
+        regroup_w(0, 1)
         bring_out(0, 0)
         transpose(1)
         bring_out(0, 1)
@@ -335,14 +335,13 @@ def tile_nestedtensorblock_pa_kernel(tc, x, ln1_g, ln1_b, w_qkv, b_qkv, out):
         multiply(0, 4)
         quantise_w(1)
         multiply(0, 5)
-        for n in (2, 3):
-            regroup_w(n, 0)
-            regroup_w(n, 1)
-        for n in (4, 5):
+        for n in (2, 4):
             regroup_w(n, 0)
             regroup_w(n, 1)
         for n in range(1, CHUNKS):
             for m in range(TOKEN_TILES):
                 multiply(n, m)
+                if n in (1, 2) and m in (1, 4):
+                    regroup_w(2 * n + 1, m // 4)
                 if m == QUANT_AT and n + 1 < CHUNKS:
                     quantise_w(n + 1)

@@ -38,6 +38,7 @@ W_ENGINE = "vsssgs"
 G_COLS = 128
 SCALAR_BANKS = [(3, 2), (3, 5), (4, 1), (4, 4), (5, 0), (5, 2)]
 STORE_LAG = 2
+LAST_PIECES = 2
 QUANT_AT = 2
 W_LOADS = [(0, 1), (1, 1), (2, 2), (4, 2)]
 
@@ -103,7 +104,11 @@ def tile_nestedtensorblock_pa_kernel(tc, x, ln1_g, ln1_b, w_qkv, b_qkv, out):
 
         nc.scalar.dma_start(out=gain_bias_in[0:K_BLOCKS, :], in_=ln1_g.rearrange("(i p) -> i p", p=P))
         nc.scalar.dma_start(out=gain_bias_in[K_BLOCKS:, :], in_=ln1_b.rearrange("(i p) -> i p", p=P))
-        load_x(0)
+        for s in range(K // BN_COLS):
+            nc.sync.dma_start(
+                out=x_sb[:, 0, s * BN_COLS : (s + 1) * BN_COLS],
+                in_=x[0:P, s * BN_COLS : (s + 1) * BN_COLS],
+            )
         load_x(1)
         load_x(2)
         load_x(3)
@@ -216,7 +221,7 @@ def tile_nestedtensorblock_pa_kernel(tc, x, ln1_g, ln1_b, w_qkv, b_qkv, out):
         w_grouped = {}
 
         def copy_on_gpsimd(out, in_):
-            nc.gpsimd.tensor_copy(out=out, in_=in_)
+            nc.gpsimd.tensor_scalar(out=out, in0=in_, scalar1=1.0, scalar2=0.0, op0=ALU.mult, op1=ALU.add)
 
         def regroup_w(n, c, pieces=None):
             if n not in w_grouped:
@@ -266,8 +271,19 @@ def tile_nestedtensorblock_pa_kernel(tc, x, ln1_g, ln1_b, w_qkv, b_qkv, out):
                 nc.gpsimd.tensor_tensor(out=result[:], in0=plain[:], in1=bias_bc[:, cols], op=ALU.add)
                 waiting.append([STORE_LAG, n, m, result])
             else:
-                nc.vector.tensor_tensor(out=result[:], in0=acc[:], in1=bias_bc[:, cols], op=ALU.add)
-                store(n, m, result)
+                pieces = LAST_PIECES if (n, m) == (CHUNKS - 1, TOKEN_TILES - 1) else 1
+                width = CHUNK // pieces
+                for q in range(0, CHUNK, width):
+                    first = n * CHUNK + q
+                    nc.vector.tensor_tensor(
+                        out=result[:, q : q + width],
+                        in0=acc[:, q : q + width],
+                        in1=bias_bc[:, first : first + width],
+                        op=ALU.add,
+                    )
+                    nc.sync.dma_start(
+                        out=out[m * P : (m + 1) * P, first : first + width], in_=result[:, q : q + width]
+                    )
             for w in list(waiting):
                 w[0] -= 1
                 if w[0] < 0 or (n, m) == (CHUNKS - 1, TOKEN_TILES - 1):

@@ -36,10 +36,10 @@ SCALAR_STATS = [1, 3]
 GPSIMD_NORM = []
 W_ENGINE = "vsssgs"
 G_COLS = 128
-SCALAR_BANKS = [(3, 2), (3, 5), (4, 1), (4, 4), (5, 0), (5, 2)]
+SCALAR_BANKS = [(3, 0), (3, 2), (3, 4), (4, 1), (4, 3), (5, 0), (5, 2)]
 STORE_LAG = 2
 LAST_PIECES = 2
-QUANT_AT = 2
+QUANT_AT = 1
 W_LOADS = [(0, 1), (1, 1), (2, 2), (4, 2)]
 
 FLOPS = 2 * TOKENS * K * N

@@ -30,6 +30,7 @@ CHUNK = 512
 CHUNKS = N // CHUNK
 LOAD_COLS = 1024
 CHUNKS_PER_LOAD = LOAD_COLS // CHUNK
+SCALAR_RUN = 8
 RUN = 4
 
 SCALAR_STATS = [1, 3]
@@ -45,10 +46,10 @@ W_LOADS = [(0, 1), (1, 1), (2, 2), (4, 2)]
 FLOPS = 2 * TOKENS * K * N
 
 
-def regroup(copy, grouped, planes):
+def regroup(copy, grouped, planes, run=RUN):
     copy(
-        out=grouped.rearrange("p (a i) t -> p a t i", i=RUN),
-        in_=planes.rearrange("p t (a i) -> p a t i", i=RUN),
+        out=grouped.rearrange("p (a i) t -> p a t i", i=run),
+        in_=planes.rearrange("p t (a i) -> p a t i", i=run),
     )
 
 
@@ -233,7 +234,12 @@ def tile_nestedtensorblock_pa_kernel(tc, x, ln1_g, ln1_b, w_qkv, b_qkv, out):
             width = G_COLS if e == "g" else CHUNK
             for i, q in enumerate(range(0, CHUNK, width)):
                 if pieces is None or i in pieces:
-                    regroup(copy, w_grouped[n][:, c, q : q + width, :], raw[:, c, :, first + q : first + q + width])
+                    regroup(
+                        copy,
+                        w_grouped[n][:, c, q : q + width, :],
+                        raw[:, c, :, first + q : first + q + width],
+                        SCALAR_RUN if e == "s" else RUN,
+                    )
 
         def quantise_w(n):
             nc.vector.quantize_mx(

from contextlib import ExitStack

import concourse.mybir as mybir
from concourse.masks import make_identity

F32 = mybir.dt.float32
BF16 = mybir.dt.bfloat16
U32 = mybir.dt.uint32
U8 = mybir.dt.uint8
FP8X4 = mybir.dt.float8_e4m3fn_x4
ALU = mybir.AluOpType
ACT = mybir.ActivationFunctionType

P = 128
PACK = 4
K_PASS = P * PACK
TOKENS = 768
K = 1024
N = 3072
EPS = 1e-5

TOKEN_TILES = TOKENS // P
PAIR = 2
GROUPS = TOKEN_TILES // PAIR
GROUP_TOKENS = PAIR * P
K_PASSES = K // K_PASS
K_BLOCKS = K // P
BN_COLS = 512
CHUNK = 512
CHUNKS = N // CHUNK
LOAD_COLS = 1024
CHUNKS_PER_LOAD = LOAD_COLS // CHUNK
SCALAR_RUN = 8
RUN = 4

SCALAR_STATS = [1, 3]
GPSIMD_NORM = []
W_ENGINE = "vsssgs"
G_COLS = 128
SCALAR_BANKS = [(3, 0), (3, 2), (3, 4), (4, 1), (4, 3), (5, 0), (5, 2)]
STORE_LAG = 2
LAST_PIECES = 2
QUANT_AT = 1
W_LOADS = [(0, 1), (1, 1), (2, 2), (4, 2)]

FLOPS = 2 * TOKENS * K * N


def regroup(copy, grouped, planes, run=RUN):
    copy(
        out=grouped.rearrange("p (a i) t -> p a t i", i=run),
        in_=planes.rearrange("p t (a i) -> p a t i", i=run),
    )


def tile_nestedtensorblock_pa_kernel(tc, x, ln1_g, ln1_b, w_qkv, b_qkv, out):
    nc = tc.nc
    with ExitStack() as ctx:
        keep = ctx.enter_context(tc.tile_pool(name="keep", bufs=1))
        stage = ctx.enter_context(tc.tile_pool(name="stage", bufs=4))
        results = ctx.enter_context(tc.tile_pool(name="results", bufs=14))
        sums = ctx.enter_context(tc.tile_pool(name="sums", bufs=4))
        psum = ctx.enter_context(tc.psum_pool(name="psum", bufs=8))

        x_sb = keep.tile([P, TOKEN_TILES, K], BF16)
        w_raw = {}
        bias_bc = keep.tile([P, N], BF16)
        gain_bias_in = keep.tile([2 * K_BLOCKS, P], BF16)
        gain_bias_rows = keep.tile([P, P], F32)
        gain_bias = keep.tile([P, 2 * K_BLOCKS], F32)
        ident = keep.tile([P, P], F32)
        eps_col = keep.tile([P, 1], F32)
        warm = keep.tile([P, 1], F32)
        stats = keep.tile([P, TOKEN_TILES, K // BN_COLS, 6], F32)
        mean_var = keep.tile([P, TOKEN_TILES, 8], F32)
        rstd = keep.tile([P, TOKEN_TILES, 8], F32)
        total = keep.tile([P, TOKEN_TILES, 8], F32)
        neg_mean = keep.tile([P, TOKEN_TILES, 8], F32)
        sum_sq = keep.tile([P, TOKEN_TILES, 8], F32)
        unread = keep.tile([P, len(SCALAR_STATS), 2, K], BF16)
        xn = keep.tile([P, TOKEN_TILES, K], F32)
        h_planes = keep.tile([P, K_BLOCKS, TOKENS], BF16)
        h_grouped = keep.tile([P, GROUPS, K_PASSES, GROUP_TOKENS, PACK], BF16, align_bytes=64)
        h_codes = keep.tile([P, GROUPS, K_PASSES, GROUP_TOKENS], U32, align_bytes=64)
        h_scales = keep.tile([P, GROUPS, K_PASSES, GROUP_TOKENS], U8, align_bytes=64)
        w_codes = keep.tile([P, CHUNKS, K_PASSES, CHUNK], U32, align_bytes=64)
        w_scales = keep.tile([P, CHUNKS, K_PASSES, CHUNK], U8, align_bytes=64)

        def load_x(i):
            nc.sync.dma_start(out=x_sb[:, i, :], in_=x[i * P : (i + 1) * P, :])

        def load_w(first, chunks, passes):
            if first not in w_raw:
                raw = keep.tile([P, K_PASSES, PACK, chunks * CHUNK], BF16, name="raw_%d" % first)
                for n in range(chunks):
                    w_raw[first + n] = (raw, n * CHUNK)
            raw = w_raw[first][0]
            for c in passes:
                nc.sync.dma_start(
                    out=raw[:, c, :, :],
                    in_=w_qkv[
                        c * K_PASS : (c + 1) * K_PASS, first * CHUNK : (first + chunks) * CHUNK
                    ].rearrange("(t p) n -> p t n", p=P),
                )

        nc.scalar.dma_start(out=gain_bias_in[0:K_BLOCKS, :], in_=ln1_g.rearrange("(i p) -> i p", p=P))
        nc.scalar.dma_start(out=gain_bias_in[K_BLOCKS:, :], in_=ln1_b.rearrange("(i p) -> i p", p=P))
        for s in range(K // BN_COLS):
            nc.sync.dma_start(
                out=x_sb[:, 0, s * BN_COLS : (s + 1) * BN_COLS],
                in_=x[0:P, s * BN_COLS : (s + 1) * BN_COLS],
            )
        load_x(1)
        load_x(2)
        load_x(3)
        load_x(4)
        load_x(5)
        load_w(0, 1, [0, 1])
        load_w(1, 1, [0, 1])
        nc.sync.dma_start(out=bias_bc[:], in_=b_qkv.partition_broadcast(P))
        load_w(2, 2, [0, 1])
        load_w(4, 2, [0, 1])

        nc.vector.memset(eps_col[:], EPS)
        nc.vector.memset(gain_bias_rows[:], 0.0)
        nc.scalar.activation(out=warm[:], in_=eps_col[:], func=ACT.Abs_reciprocal_sqrt)
        make_identity(nc, ident[:])

        def spread_gain_and_bias():
            nc.vector.tensor_copy(out=gain_bias_rows[0 : 2 * K_BLOCKS, :], in_=gain_bias_in[:])
            gb_bank = psum.tile([P, CHUNK], F32, tag="bank")
            nc.tensor.transpose(gb_bank[:, 0:P], gain_bias_rows[:], ident[:])
            nc.scalar.copy(out=gain_bias[:], in_=gb_bank[:, 0 : 2 * K_BLOCKS])

        def statistics(i, s):
            nc.vector.bn_stats(out=stats[:, i, s, :], in_=x_sb[:, i, s * BN_COLS : (s + 1) * BN_COLS])

        def aggregate(i):
            nc.vector.bn_aggr(
                out=mean_var[:, i, 0:2], in_=stats[:, i, :, :].rearrange("p s v -> p (s v)")
            )

        def root(i):
            own = i in SCALAR_STATS
            nc.scalar.activation(
                out=rstd[:, i, 0:1],
                in_=sum_sq[:, i, 0:1] if own else mean_var[:, i, 1:2],
                func=ACT.Abs_reciprocal_sqrt,
                bias=eps_col[:, 0:1],
                scale=1.0 / K if own else 1.0,
            )

        def scalar_sum(i):
            nc.scalar.activation(
                out=unread[:, SCALAR_STATS.index(i), 0, :],
                in_=x_sb[:, i, :],
                func=ACT.Identity,
                accum_out=total[:, i, 0:1],
            )
            nc.scalar.activation(
                out=neg_mean[:, i, 0:1], in_=total[:, i, 0:1], func=ACT.Copy, scale=-1.0 / K
            )

        def scalar_squares(i):
            nc.scalar.activation(
                out=unread[:, SCALAR_STATS.index(i), 1, :],
                in_=x_sb[:, i, :],
                func=ACT.Square,
                bias=neg_mean[:, i, 0:1],
                accum_out=sum_sq[:, i, 0:1],
            )

        def normalise(i):
            engine = nc.gpsimd if i in GPSIMD_NORM else nc.vector
            own = i in SCALAR_STATS
            engine.tensor_scalar(
                out=xn[:, i, :],
                in0=x_sb[:, i, :],
                scalar1=neg_mean[:, i, 0:1] if own else mean_var[:, i, 0:1],
                scalar2=rstd[:, i, 0:1],
                op0=ALU.add if own else ALU.subtract,
                op1=ALU.mult,
            )

        h_banks = {}

        def transpose(g):
            for kb in range(0, K_BLOCKS, 2):
                bank = psum.tile([P, CHUNK], F32, tag="bank")
                h_banks[(g, kb)] = bank
                for b in range(2):
                    for j in range(PAIR):
                        nc.tensor.transpose(
                            bank[:, (b * PAIR + j) * P : (b * PAIR + j + 1) * P],
                            xn[:, g * PAIR + j, (kb + b) * P : (kb + b + 1) * P],
                            ident[:],
                        )

        def bring_out(g, c):
            for k in range(c * PACK, (c + 1) * PACK):
                o = h_planes[:, k, g * GROUP_TOKENS : (g + 1) * GROUP_TOKENS]
                half = (k % 2) * GROUP_TOKENS
                i = h_banks[(g, k - k % 2)][:, half : half + GROUP_TOKENS]
                gain = gain_bias[:, k : k + 1]
                bias = gain_bias[:, K_BLOCKS + k : K_BLOCKS + k + 1]
                nc.scalar.activation(out=o, in_=i, func=ACT.Identity, bias=bias, scale=gain)

        def regroup_h(g, c):
            regroup(
                nc.vector.tensor_copy,
                h_grouped[:, g, c, :, :],
                h_planes[:, c * PACK : (c + 1) * PACK, g * GROUP_TOKENS : (g + 1) * GROUP_TOKENS],
            )

        def quantise_h(g):
            nc.vector.quantize_mx(
                out=h_codes[:, g, :, :].rearrange("p c n -> p (c n)").bitcast(FP8X4),
                scales=h_scales[:, g, :, :].rearrange("p c n -> p (c n)"),
                in_=h_grouped[:, g, :, :, :].rearrange("p c n t -> p (c n t)"),
            )

        w_grouped = {}

        def copy_on_gpsimd(out, in_):
            nc.gpsimd.tensor_scalar(out=out, in0=in_, scalar1=1.0, scalar2=0.0, op0=ALU.mult, op1=ALU.add)

        def regroup_w(n, c, pieces=None):
            if n not in w_grouped:
                grouped = stage.tile([P, K_PASSES, CHUNK, PACK], BF16, align_bytes=64, tag="w_grouped")
                w_grouped[n] = grouped
            raw, first = w_raw[n]
            e = W_ENGINE[n]
            copy = {"v": nc.vector.tensor_copy, "s": nc.scalar.copy, "g": copy_on_gpsimd}[e]
            width = G_COLS if e == "g" else CHUNK
            for i, q in enumerate(range(0, CHUNK, width)):
                if pieces is None or i in pieces:
                    regroup(
                        copy,
                        w_grouped[n][:, c, q : q + width, :],
                        raw[:, c, :, first + q : first + q + width],
                        SCALAR_RUN if e == "s" else RUN,
                    )

        def quantise_w(n):
            nc.vector.quantize_mx(
                out=w_codes[:, n, :, :].rearrange("p c n -> p (c n)").bitcast(FP8X4),
                scales=w_scales[:, n, :, :].rearrange("p c n -> p (c n)"),
                in_=w_grouped[n][:].rearrange("p c n t -> p (c n t)"),
            )

        waiting = []

        def store(n, m, result):
            nc.sync.dma_start(
                out=out[m * P : (m + 1) * P, n * CHUNK : (n + 1) * CHUNK], in_=result[:]
            )

        def multiply(n, m):
            g, j = divmod(m, PAIR)
            tokens = slice(j * P, (j + 1) * P)
            cols = slice(n * CHUNK, (n + 1) * CHUNK)
            acc = psum.tile([P, CHUNK], F32, tag="bank")
            for c in range(K_PASSES):
                nc.tensor.matmul_mx(
                    out=acc[:],
                    lhsT=h_codes[:, g, c, tokens].bitcast(FP8X4),
                    lhsT_scale=h_scales[:, g, c, tokens],
                    rhs=w_codes[:, n, c, :].bitcast(FP8X4),
                    rhs_scale=w_scales[:, n, c, :],
                    start=(c == 0),
                    stop=(c == K_PASSES - 1),
                )
            result = results.tile([P, CHUNK], F32)
            if (n, m) in SCALAR_BANKS:
                plain = sums.tile([P, CHUNK], F32)
                nc.scalar.copy(out=plain[:], in_=acc[:])
                nc.gpsimd.tensor_tensor(out=result[:], in0=plain[:], in1=bias_bc[:, cols], op=ALU.add)
                waiting.append([STORE_LAG, n, m, result])
            else:
                pieces = LAST_PIECES if (n, m) == (CHUNKS - 1, TOKEN_TILES - 1) else 1
                width = CHUNK // pieces
                for q in range(0, CHUNK, width):
                    first = n * CHUNK + q
                    nc.vector.tensor_tensor(
                        out=result[:, q : q + width],
                        in0=acc[:, q : q + width],
                        in1=bias_bc[:, first : first + width],
                        op=ALU.add,
                    )
                    nc.sync.dma_start(
                        out=out[m * P : (m + 1) * P, first : first + width], in_=result[:, q : q + width]
                    )
            for w in list(waiting):
                w[0] -= 1
                if w[0] < 0 or (n, m) == (CHUNKS - 1, TOKEN_TILES - 1):
                    store(*w[1:])
                    waiting.remove(w)

        def both_statistics(i):
            for s in range(K // BN_COLS):
                statistics(i, s)

        both_statistics(0)
        scalar_sum(1)
        aggregate(0)
        root(0)
        normalise(0)
        both_statistics(2)
        spread_gain_and_bias()
        scalar_squares(1)
        root(1)
        statistics(4, 0)
        aggregate(2)
        root(2)
        normalise(2)
        statistics(4, 1)
        normalise(1)
        transpose(0)
        scalar_sum(3)
        statistics(5, 0)
        aggregate(4)
        statistics(5, 1)
        root(4)
        normalise(4)
        scalar_squares(3)
        aggregate(5)
        root(3)
        root(5)
        normalise(3)
        normalise(5)
        regroup_w(0, 0)
        regroup_w(0, 1)
        bring_out(0, 0)
        transpose(1)
        bring_out(0, 1)
        transpose(2)
        regroup_h(0, 0)
        quantise_w(0)
        regroup_h(0, 1)
        bring_out(1, 0)
        bring_out(1, 1)
        bring_out(2, 0)
        bring_out(2, 1)
        regroup_w(1, 0)
        regroup_w(1, 1)
        regroup_h(1, 0)
        quantise_h(0)
        regroup_h(1, 1)
        multiply(0, 0)
        quantise_h(1)
        multiply(0, 1)
        regroup_h(2, 0)
        regroup_h(2, 1)
        multiply(0, 2)
        quantise_h(2)
        multiply(0, 3)
        multiply(0, 4)
        quantise_w(1)
        multiply(0, 5)
        for n in (2, 4):
            regroup_w(n, 0)
            regroup_w(n, 1)
        for n in range(1, CHUNKS):
            for m in range(TOKEN_TILES):
                multiply(n, m)
                if n in (1, 2) and m in (1, 4):
                    regroup_w(2 * n + 1, m // 4)
                if m == QUANT_AT and n + 1 < CHUNKS:
                    quantise_w(n + 1)
